import numpy as np
import ml_dtypes


def mxq(x, axis, fmt="e4m3"):
    dtype, down = {"e4m3": (ml_dtypes.float8_e4m3fn, 7), "e5m2": (ml_dtypes.float8_e5m2, 14)}[fmt]
    v = np.moveaxis(np.asarray(x, np.float32).astype(ml_dtypes.bfloat16).astype(np.float64), axis, -1)
    blocks = v.reshape(v.shape[:-1] + (-1, 32))
    amax = np.abs(blocks).max(-1, keepdims=True)
    byte = np.maximum(np.where(amax > 0, np.frexp(amax)[1] - 1 + 127, 0) - down, 1)
    scale = np.exp2(byte - 127.0)
    codes = (blocks / scale).astype(np.float32).astype(dtype).astype(np.float64)
    return np.moveaxis((codes * scale).reshape(v.shape), -1, axis)


WIDE = False


def mx_kscale(k):
    if not WIDE:
        return np.ones(k)
    levels = np.array([10, -10, 5, -5, 0])
    a = np.random.permutation(np.resize(levels, k // 512 * 4)).reshape(k // 512, 4)
    idx = np.arange(k)
    return np.exp2(a[idx // 512, idx % 128 // 32])


BF16 = ml_dtypes.bfloat16


def bf(x):
    return np.asarray(x, np.float32).astype(BF16)


def f64(x):
    return np.asarray(x).astype(np.float64)


E2M1 = np.array([0.0, 0.5, 1.0, 1.5, 2.0, 3.0, 4.0, 6.0, -0.0, -0.5, -1.0, -1.5, -2.0, -3.0, -4.0, -6.0])


def pack_weight(w, fmt):
    k, n = w.shape
    w = f64(bf(w)).reshape(k // 32, 32, n)
    amax = np.abs(w).max(1)
    if fmt == "e4m3":
        byte = np.frexp(amax)[1] - 1 + 127 - 7
    else:
        mant, ex = np.frexp(amax / 6.0)
        byte = np.where(mant > 0.5, ex, ex - 1) + 127
    byte = np.clip(np.where(amax > 0, byte, 1), 1, 254)
    scaled = (w * np.exp2(127.0 - byte)[:, None, :]).reshape(k, n).astype(np.float32)
    by_word = np.ascontiguousarray(scaled.reshape(k // 512, 128, 4, n).transpose(0, 1, 3, 2))
    if fmt == "e4m3":
        words = by_word.astype(ml_dtypes.float8_e4m3fn).view(np.uint8)
    else:
        c = by_word.astype(ml_dtypes.float4_e2m1fn).view(np.uint8) & 0xF
        words = c[..., 0::2] | (c[..., 1::2] << 4)
    return np.ascontiguousarray(words), np.ascontiguousarray(byte.astype(np.uint8).reshape(k // 512, 16, n))


def unpack_weight(words, scales, fmt):
    g, p, n, _ = words.shape
    if fmt == "e4m3":
        vals = np.ascontiguousarray(words).view(ml_dtypes.float8_e4m3fn).astype(np.float64)
    else:
        nib = np.empty((g, p, n, 4), np.uint8)
        nib[..., 0::2] = words & 0xF
        nib[..., 1::2] = words >> 4
        vals = E2M1[nib]
    vals = vals * np.repeat(np.exp2(scales.astype(np.float64) - 127.0), 8, axis=1)[..., None]
    return vals.transpose(0, 1, 3, 2).reshape(g * 512, n)


B, F, H1, E, N, P, L, C, S = 2048, 2048, 512, 512, 32, 8, 100, 16, 100
EPS = 1e-5


def layernorm(x, g, b):
    mu = x.mean(axis=-1, keepdims=True)
    var = x.var(axis=-1, keepdims=True)
    return (x - mu) / np.sqrt(var + EPS) * g + b


def setup_inputs():
    rn = np.random.standard_normal
    s = mx_kscale(H1)
    t = mx_kscale(E)
    h1 = bf(np.maximum(rn((B, H1)), 0.0) * s)
    W2_words, W2_scales = pack_weight(rn((H1, E)) / np.sqrt(H1) / s[:, None], "e4m3")
    return {"h1": h1,
            "W2_words": W2_words,
            "W2_scales": W2_scales,
            "b2": bf(rn(E) * 0.3),
            "ln_g": bf((1.0 + 0.2 * rn(E)) * t),
            "ln_b": bf(0.3 * rn(E) * t),
            "pc_W": bf(rn((N, E, P)) / np.sqrt(E) / t[None, :, None]),
            "pc_b": bf(0.3 * rn((N, P))),
            "pc_g": bf(1.0 + 0.2 * rn((N, P))),
            "pc_beta": bf(0.3 * rn((N, P)))}


def reference(h1, W2_words, W2_scales, b2, ln_g, ln_b, pc_W, pc_b, pc_g, pc_beta):
    z = np.maximum((mxq(f64(h1), 1, "e4m3") @ unpack_weight(W2_words, W2_scales, "e4m3")) + f64(b2), 0.0)
    h = layernorm(z, f64(ln_g), f64(ln_b))
    w = mxq(f64(pc_W), 1, "e4m3").transpose(1, 0, 2).reshape(E, N * P)
    prim = (mxq(h, 1, "e4m3") @ w).reshape(B, N, P) + f64(pc_b)[None]
    return layernorm(prim, f64(pc_g)[None], f64(pc_beta)[None])

@@ -1,0 +1,346 @@
+from contextlib import ExitStack
+
+import concourse.mybir as mybir
+from concourse.masks import make_identity
+
+F32 = mybir.dt.float32
+BF16 = mybir.dt.bfloat16
+I32 = mybir.dt.int32
+U32 = mybir.dt.uint32
+U8 = mybir.dt.uint8
+FP8X4 = mybir.dt.float8_e4m3fn_x4
+ALU = mybir.AluOpType
+ACT = mybir.ActivationFunctionType
+AXIS = mybir.AxisListType
+
+P = 128
+PACK = 4
+B, H1, E = 2048, 512, 512
+CAPS, CAP_DIM = 32, 8
+NP = CAPS * CAP_DIM
+NP_TILES = NP // P
+TILES = B // P
+PAIR = 2
+PAIRS = TILES // PAIR
+PAIR_ROWS = PAIR * P
+GROUPS = PAIR * CAPS
+EPS = 1e-5
+
+FLOPS = 2 * B * H1 * E + 2 * B * E * NP
+
+
+def tile_hotpatchcapsmodel_pa_kernel(
+    tc, h1, W2_words, W2_scales, b2, ln_g, ln_b, pc_W, pc_b, pc_g, pc_beta, out
+):
+    nc = tc.nc
+    with ExitStack() as ctx:
+        keep = ctx.enter_context(tc.tile_pool(name="keep", bufs=1))
+        work = ctx.enter_context(tc.tile_pool(name="work", bufs=3))
+        psum = ctx.enter_context(tc.psum_pool(name="psum", bufs=1))
+        ctx.enter_context(tc.manual_schedule())
+
+        h1_rows = h1.rearrange("(p t) k -> p t k", t=TILES)
+        out_rows = out.rearrange("(p t) n q -> p t (n q)", t=TILES)
+
+        w2_plane = keep.tile([P, E], U8, align_bytes=64)
+        nc.vector.memset(w2_plane[:].bitcast(I32), 0)
+        small_rows = keep.tile([P, P], BF16)
+        nc.vector.memset(small_rows[:], 0.0)
+        eps = keep.tile([P, 1], F32)
+        nc.vector.memset(eps[:], EPS)
+
+        pw_sb = keep.tile([P, P * CAP_DIM], BF16)
+        nc.sync.dma_start(out=pw_sb[:], in_=pc_W.rearrange("n (j e) q -> (n j) (e q)", j=PACK))
+        h1_sb = keep.tile([P, TILES, H1], BF16)
+        nc.sync.dma_start(out=h1_sb[:, 0:PAIR, :], in_=h1_rows[:, 0:PAIR, :])
+        w2_codes = keep.tile([P, E], U32, align_bytes=64)
+        nc.sync.dma_start(
+            out=w2_codes[:].bitcast(I32),
+            in_=W2_words[0].rearrange("p n t -> p (n t)").bitcast(I32),
+        )
+        for quadrant in range(4):
+            nc.sync.dma_start(
+                out=w2_plane[32 * quadrant : 32 * quadrant + 4, :].bitcast(I32),
+                in_=W2_scales[0, 4 * quadrant : 4 * quadrant + 4, :].bitcast(I32),
+            )
+        for n in range(1, PAIRS):
+            nc.sync.dma_start(
+                out=h1_sb[:, PAIR * n : PAIR * (n + 1), :], in_=h1_rows[:, PAIR * n : PAIR * (n + 1), :]
+            )
+
+        b2_bc = keep.tile([P, E], BF16)
+        nc.scalar.dma_start(out=b2_bc[:], in_=b2.partition_broadcast(P))
+        nc.scalar.dma_start(out=small_rows[0:4, :], in_=ln_g.rearrange("(j c) -> j c", c=P))
+        nc.scalar.dma_start(out=small_rows[4:8, :], in_=ln_b.rearrange("(j c) -> j c", c=P))
+        nc.scalar.dma_start(out=small_rows[8:10, :], in_=pc_b.rearrange("(c n) q -> c (n q)", c=NP_TILES))
+        pcg_bc = keep.tile([P, NP], BF16)
+        nc.scalar.dma_start(out=pcg_bc[:], in_=pc_g.rearrange("n q -> (n q)").partition_broadcast(P))
+        pcbeta_bc = keep.tile([P, NP], BF16)
+        nc.scalar.dma_start(out=pcbeta_bc[:], in_=pc_beta.rearrange("n q -> (n q)").partition_broadcast(P))
+
+        warm = keep.tile([P, 1], F32)
+        nc.scalar.activation(out=warm[:], in_=eps[:], func=ACT.Abs_reciprocal_sqrt)
+
+        ident_b = keep.tile([P, P], BF16)
+        make_identity(nc, ident_b[:])
+        ident_f = keep.tile([P, P], F32)
+        make_identity(nc, ident_f[:])
+        same_capsule = keep.tile([P, P // CAP_DIM], F32)
+        nc.vector.tensor_reduce(
+            out=same_capsule[:], in_=ident_f[:].rearrange("p (n q) -> p n q", q=CAP_DIM), axis=AXIS.X, op=ALU.add
+        )
+        centre = keep.tile([P, P], F32)
+        nc.vector.scalar_tensor_tensor(
+            out=centre[:].rearrange("p (n q) -> p n q", q=CAP_DIM),
+            in0=same_capsule[:].unsqueeze(2).to_broadcast([P, P // CAP_DIM, CAP_DIM]),
+            scalar=-1.0 / CAP_DIM,
+            in1=ident_f[:].rearrange("p (n q) -> p n q", q=CAP_DIM),
+            op0=ALU.mult,
+            op1=ALU.add,
+        )
+
+        pw_t = psum.tile([P, CAP_DIM, P], BF16, tag="centred", bufs=2)
+        pw_by_q = pw_sb[:].rearrange("p (e q) -> p e q", q=CAP_DIM)
+        for q in range(CAP_DIM):
+            nc.tensor.transpose(pw_t[:, q, :], pw_by_q[:, :, q], ident_b[:])
+        pw_grouped = keep.tile([P, CAPS, CAP_DIM, PACK], BF16, align_bytes=64)
+        nc.scalar.copy(out=pw_grouped[:], in_=pw_t[:].rearrange("p q (n j) -> p n q j", j=PACK))
+        small_rows_t = psum.tile([P, P], BF16, tag="centred", bufs=2)
+        nc.tensor.transpose(small_rows_t[:], small_rows[:], ident_b[:])
+
+        h1_t, h1_grouped, h1_codes, h1_plane = {}, {}, {}, {}
+        acc, z, z_sum, neg_mean, rstd = {}, {}, {}, {}, {}
+        normed, normed_t, h_t, h_codes, h_plane = {}, {}, {}, {}, {}
+        prim_t, biased_t, centred, g_squares, g_sq_sum, g_rstd, result = {}, {}, {}, {}, {}, {}, {}
+
+        def transpose_h1(n):
+            h1_t[n] = psum.tile([P, PAIR, 2, P], F32, name="h1_t", tag="h1_t")
+            for i in range(PAIR):
+                words = h1_sb[:, PAIR * n + i, :].bitcast(F32)
+                for u in range(2):
+                    nc.tensor.transpose(h1_t[n][:, i, u, :], words[:, u : H1 // 2 : 2], ident_f[:])
+
+        def group_h1(n):
+            h1_grouped[n] = work.tile([P, PAIR, P, PACK], BF16, name="h1_grouped", align_bytes=64)
+            nc.vector.tensor_copy(
+                out=h1_grouped[n][:].bitcast(F32), in_=h1_t[n][:].rearrange("p i u r -> p i r u")
+            )
+
+        def quantise_h1(n):
+            h1_codes[n] = work.tile([P, PAIR_ROWS], U32, name="h1_codes", align_bytes=64)
+            h1_plane[n] = work.tile([P, PAIR_ROWS], U8, name="h1_plane", align_bytes=64)
+            nc.vector.quantize_mx(
+                out=h1_codes[n][:].bitcast(FP8X4),
+                scales=h1_plane[n][:],
+                in_=h1_grouped[n][:].rearrange("p i r t -> p (i r t)"),
+            )
+
+        def embed(n):
+            for i in range(PAIR):
+                rows = slice(P * i, P * (i + 1))
+                acc[n, i] = psum.tile([P, E], F32, name="acc", tag="acc", bufs=2)
+                nc.tensor.matmul_mx(
+                    out=acc[n, i][:],
+                    lhsT=h1_codes[n][:, rows].bitcast(FP8X4),
+                    lhsT_scale=h1_plane[n][:, rows],
+                    rhs=w2_codes[:].bitcast(FP8X4),
+                    rhs_scale=w2_plane[:],
+                    start=True,
+                    stop=True,
+                )
+
+        def add_b2(n):
+            z[n] = work.tile([P, PAIR, E], F32, name="z")
+            for i in range(PAIR):
+                nc.vector.tensor_tensor(out=z[n][:, i, :], in0=acc[n, i][:], in1=b2_bc[:], op=ALU.add)
+
+        def relu_and_sum(n):
+            z_sum[n] = work.tile([P, PAIR], F32, name="z_sum")
+            for i in range(PAIR):
+                nc.scalar.activation(
+                    out=z[n][:, i, :], in_=z[n][:, i, :], func=ACT.Relu, accum_out=z_sum[n][:, i : i + 1]
+                )
+
+        def mean(n):
+            neg_mean[n] = work.tile([P, PAIR], F32, name="neg_mean")
+            nc.vector.tensor_scalar(
+                out=neg_mean[n][:], in0=z_sum[n][:], scalar1=-1.0 / E, scalar2=None, op0=ALU.mult
+            )
+
+        def variance(n):
+            sq_sum = work.tile([P, PAIR], F32)
+            for i in range(PAIR):
+                squares = work.tile([P, E], BF16)
+                nc.scalar.activation(
+                    out=squares[:],
+                    in_=z[n][:, i, :],
+                    func=ACT.Square,
+                    bias=neg_mean[n][:, i : i + 1],
+                    scale=1.0,
+                    accum_out=sq_sum[:, i : i + 1],
+                )
+            rstd[n] = work.tile([P, PAIR], F32, name="rstd")
+            nc.scalar.activation(
+                out=rstd[n][:], in_=sq_sum[:], func=ACT.Abs_reciprocal_sqrt, bias=eps[:], scale=1.0 / E
+            )
+
+        def normalise(n):
+            normed[n] = work.tile([P, PAIR, E], F32, name="normed")
+            for i in range(PAIR):
+                nc.vector.tensor_scalar(
+                    out=normed[n][:, i, :],
+                    in0=z[n][:, i, :],
+                    scalar1=neg_mean[n][:, i : i + 1],
+                    scalar2=rstd[n][:, i : i + 1],
+                    op0=ALU.add,
+                    op1=ALU.mult,
+                )
+
+        def transpose_normed(n):
+            for half in range(2):
+                normed_t[n, half] = psum.tile([P, 2, PAIR, P], F32, name="normed_t", tag="normed_t", bufs=2)
+                for jj in range(2):
+                    j = 2 * half + jj
+                    for i in range(PAIR):
+                        nc.tensor.transpose(
+                            normed_t[n, half][:, jj, i, :], normed[n][:, i, P * j : P * (j + 1)], ident_f[:]
+                        )
+
+        def gain_and_shift(n):
+            h_t[n] = work.tile([P, PACK, PAIR_ROWS], BF16, name="h_t")
+            for j in range(PACK):
+                nc.scalar.activation(
+                    out=h_t[n][:, j, :],
+                    in_=normed_t[n, j // 2][:, j % 2, :, :].rearrange("p i r -> p (i r)"),
+                    func=ACT.Identity,
+                    bias=columns[:, PACK + j : PACK + j + 1],
+                    scale=columns[:, j : j + 1],
+                )
+
+        def quantise_h(n):
+            h_grouped = work.tile([P, PAIR_ROWS, PACK], BF16, align_bytes=64)
+            nc.vector.tensor_copy(
+                out=h_grouped[:].rearrange("p (c x) j -> p c j x", x=4),
+                in_=h_t[n][:].rearrange("p j (c x) -> p c j x", x=4),
+            )
+            h_codes[n] = work.tile([P, PAIR_ROWS], U32, name="h_codes", align_bytes=64)
+            h_plane[n] = work.tile([P, PAIR_ROWS], U8, name="h_plane", align_bytes=64)
+            nc.vector.quantize_mx(
+                out=h_codes[n][:].bitcast(FP8X4),
+                scales=h_plane[n][:],
+                in_=h_grouped[:].rearrange("p r j -> p (r j)"),
+            )
+
+        def capsules(n):
+            prim_t[n] = psum.tile([P, NP_TILES, PAIR_ROWS], F32, name="prim_t", tag="prim_t")
+            for c in range(NP_TILES):
+                cols = slice(P * c, P * (c + 1))
+                nc.tensor.matmul_mx(
+                    out=prim_t[n][:, c, :],
+                    lhsT=pw_codes[:, cols].bitcast(FP8X4),
+                    lhsT_scale=pw_plane[:, cols],
+                    rhs=h_codes[n][:].bitcast(FP8X4),
+                    rhs_scale=h_plane[n][:],
+                    start=True,
+                    stop=True,
+                )
+
+        def add_pc_b(n):
+            biased_t[n] = work.tile([P, NP_TILES, PAIR_ROWS], F32, name="biased_t")
+            for c in range(NP_TILES):
+                nc.scalar.activation(
+                    out=biased_t[n][:, c, :],
+                    in_=prim_t[n][:, c, :],
+                    func=ACT.Identity,
+                    bias=columns[:, 2 * PACK + c : 2 * PACK + c + 1],
+                    scale=1.0,
+                )
+
+        def centre_and_transpose(n):
+            centred[n] = psum.tile([P, PAIR, NP], F32, name="centred", tag="centred", bufs=2)
+            for i in range(PAIR):
+                for c in range(NP_TILES):
+                    nc.tensor.matmul(
+                        out=centred[n][:, i, P * c : P * (c + 1)],
+                        lhsT=biased_t[n][:, c, P * i : P * (i + 1)],
+                        rhs=centre[:],
+                        start=True,
+                        stop=True,
+                    )
+
+        def square(n):
+            g_squares[n] = work.tile([P, GROUPS, CAP_DIM], F32, name="g_squares")
+            nc.scalar.activation(
+                out=g_squares[n][:].rearrange("p g q -> p (g q)"),
+                in_=centred[n][:].rearrange("p i c -> p (i c)"),
+                func=ACT.Square,
+            )
+
+        def sum_squares(n):
+            g_sq_sum[n] = work.tile([P, GROUPS], F32, name="g_sq_sum")
+            nc.vector.tensor_reduce(out=g_sq_sum[n][:], in_=g_squares[n][:], axis=AXIS.X, op=ALU.add)
+
+        def capsule_rstd(n):
+            g_rstd[n] = work.tile([P, GROUPS], F32, name="g_rstd")
+            nc.scalar.activation(
+                out=g_rstd[n][:], in_=g_sq_sum[n][:], func=ACT.Abs_reciprocal_sqrt, bias=eps[:], scale=1.0 / CAP_DIM
+            )
+
+        def scale_capsules(n):
+            result[n] = work.tile([P, PAIR, NP], F32, name="result")
+            nc.vector.tensor_tensor(
+                out=result[n][:].rearrange("p i (n q) -> p (i n) q", q=CAP_DIM),
+                in0=centred[n][:].rearrange("p i (n q) -> p (i n) q", q=CAP_DIM),
+                in1=g_rstd[n][:].unsqueeze(2).to_broadcast([P, GROUPS, CAP_DIM]),
+                op=ALU.mult,
+            )
+
+        def finish(n):
+            over_pair = [P, PAIR, NP]
+            nc.gpsimd.tensor_tensor(
+                out=result[n][:], in0=result[n][:], in1=pcg_bc[:].unsqueeze(1).to_broadcast(over_pair), op=ALU.mult
+            )
+            nc.gpsimd.tensor_tensor(
+                out=result[n][:], in0=result[n][:], in1=pcbeta_bc[:].unsqueeze(1).to_broadcast(over_pair), op=ALU.add
+            )
+            nc.sync.dma_start(out=out_rows[:, PAIR * n : PAIR * (n + 1), :], in_=result[n][:])
+
+        def run(stage, n):
+            if 0 <= n < PAIRS:
+                stage(n)
+
+        transpose_h1(0)
+        group_h1(0)
+        quantise_h1(0)
+        pw_codes = keep.tile([P, NP], U32, align_bytes=64)
+        pw_plane = keep.tile([P, NP], U8, align_bytes=64)
+        nc.vector.quantize_mx(
+            out=pw_codes[:].bitcast(FP8X4),
+            scales=pw_plane[:],
+            in_=pw_grouped[:].rearrange("p n q j -> p (n q j)"),
+        )
+        columns = keep.tile([P, 2 * PACK + NP_TILES], F32)
+        nc.vector.tensor_copy(out=columns[:], in_=small_rows_t[:, 0 : 2 * PACK + NP_TILES])
+        embed(0)
+
+        for n in range(PAIRS + 3):
+            run(transpose_h1, n + 1)
+            run(add_b2, n)
+            run(relu_and_sum, n)
+            run(quantise_h, n - 1)
+            run(capsules, n - 1)
+            run(mean, n)
+            run(group_h1, n + 1)
+            run(capsule_rstd, n - 3)
+            run(scale_capsules, n - 3)
+            run(finish, n - 3)
+            run(variance, n)
+            run(quantise_h1, n + 1)
+            run(embed, n + 1)
+            run(square, n - 2)
+            run(normalise, n)
+            run(transpose_normed, n)
+            run(sum_squares, n - 2)
+            run(add_pc_b, n - 1)
+            run(centre_and_transpose, n - 1)
+            run(gain_and_shift, n)

@@ -35,9 +35,8 @@ def tile_hotpatchcapsmodel_pa_kernel(
     nc = tc.nc
     with ExitStack() as ctx:
         keep = ctx.enter_context(tc.tile_pool(name="keep", bufs=1))
-        work = ctx.enter_context(tc.tile_pool(name="work", bufs=3))
+        work = ctx.enter_context(tc.tile_pool(name="work", bufs=4))
         psum = ctx.enter_context(tc.psum_pool(name="psum", bufs=1))
-        ctx.enter_context(tc.manual_schedule())
 
         h1_rows = h1.rearrange("(p t) k -> p t k", t=TILES)
         out_rows = out.rearrange("(p t) n q -> p t (n q)", t=TILES)
@@ -305,13 +304,6 @@ def tile_hotpatchcapsmodel_pa_kernel(
             )
             nc.sync.dma_start(out=out_rows[:, PAIR * n : PAIR * (n + 1), :], in_=result[n][:])
 
-        def run(stage, n):
-            if 0 <= n < PAIRS:
-                stage(n)
-
-        transpose_h1(0)
-        group_h1(0)
-        quantise_h1(0)
         pw_codes = keep.tile([P, NP], U32, align_bytes=64)
         pw_plane = keep.tile([P, NP], U8, align_bytes=64)
         nc.vector.quantize_mx(
@@ -321,26 +313,25 @@ def tile_hotpatchcapsmodel_pa_kernel(
         )
         columns = keep.tile([P, 2 * PACK + NP_TILES], F32)
         nc.vector.tensor_copy(out=columns[:], in_=small_rows_t[:, 0 : 2 * PACK + NP_TILES])
-        embed(0)
 
-        for n in range(PAIRS + 3):
-            run(transpose_h1, n + 1)
-            run(add_b2, n)
-            run(relu_and_sum, n)
-            run(quantise_h, n - 1)
-            run(capsules, n - 1)
-            run(mean, n)
-            run(group_h1, n + 1)
-            run(capsule_rstd, n - 3)
-            run(scale_capsules, n - 3)
-            run(finish, n - 3)
-            run(variance, n)
-            run(quantise_h1, n + 1)
-            run(embed, n + 1)
-            run(square, n - 2)
-            run(normalise, n)
-            run(transpose_normed, n)
-            run(sum_squares, n - 2)
-            run(add_pc_b, n - 1)
-            run(centre_and_transpose, n - 1)
-            run(gain_and_shift, n)
+        for n in range(PAIRS):
+            transpose_h1(n)
+            group_h1(n)
+            quantise_h1(n)
+            embed(n)
+            add_b2(n)
+            relu_and_sum(n)
+            mean(n)
+            variance(n)
+            normalise(n)
+            transpose_normed(n)
+            gain_and_shift(n)
+            quantise_h(n)
+            capsules(n)
+            add_pc_b(n)
+            centre_and_transpose(n)
+            square(n)
+            sum_squares(n)
+            capsule_rstd(n)
+            scale_capsules(n)
+            finish(n)

@@ -20,7 +20,7 @@ CAPS, CAP_DIM = 32, 8
 NP = CAPS * CAP_DIM
 NP_TILES = NP // P
 TILES = B // P
-PAIR = 2
+PAIR = 1
 PAIRS = TILES // PAIR
 PAIR_ROWS = PAIR * P
 GROUPS = PAIR * CAPS

@@ -296,10 +296,10 @@ def tile_hotpatchcapsmodel_pa_kernel(
 
         def finish(n):
             over_pair = [P, PAIR, NP]
-            nc.gpsimd.tensor_tensor(
+            nc.vector.tensor_tensor(
                 out=result[n][:], in0=result[n][:], in1=pcg_bc[:].unsqueeze(1).to_broadcast(over_pair), op=ALU.mult
             )
-            nc.gpsimd.tensor_tensor(
+            nc.vector.tensor_tensor(
                 out=result[n][:], in0=result[n][:], in1=pcbeta_bc[:].unsqueeze(1).to_broadcast(over_pair), op=ALU.add
             )
             nc.sync.dma_start(out=out_rows[:, PAIR * n : PAIR * (n + 1), :], in_=result[n][:])

@@ -20,10 +20,6 @@ CAPS, CAP_DIM = 32, 8
 NP = CAPS * CAP_DIM
 NP_TILES = NP // P
 TILES = B // P
-PAIR = 1
-PAIRS = TILES // PAIR
-PAIR_ROWS = PAIR * P
-GROUPS = PAIR * CAPS
 EPS = 1e-5
 
 FLOPS = 2 * B * H1 * E + 2 * B * E * NP
@@ -43,15 +39,15 @@ def tile_hotpatchcapsmodel_pa_kernel(
 
         w2_plane = keep.tile([P, E], U8, align_bytes=64)
         nc.vector.memset(w2_plane[:].bitcast(I32), 0)
-        small_rows = keep.tile([P, P], BF16)
-        nc.vector.memset(small_rows[:], 0.0)
+        b2_rows = keep.tile([P, P], BF16)
+        nc.vector.memset(b2_rows[:], 0.0)
+        other_rows = keep.tile([P, P], BF16)
+        nc.vector.memset(other_rows[:], 0.0)
         eps = keep.tile([P, 1], F32)
         nc.vector.memset(eps[:], EPS)
 
-        pw_sb = keep.tile([P, P * CAP_DIM], BF16)
-        nc.sync.dma_start(out=pw_sb[:], in_=pc_W.rearrange("n (j e) q -> (n j) (e q)", j=PACK))
         h1_sb = keep.tile([P, TILES, H1], BF16)
-        nc.sync.dma_start(out=h1_sb[:, 0:PAIR, :], in_=h1_rows[:, 0:PAIR, :])
+        nc.sync.dma_start(out=h1_sb[:, 0:2, :], in_=h1_rows[:, 0:2, :])
         w2_codes = keep.tile([P, E], U32, align_bytes=64)
         nc.sync.dma_start(
             out=w2_codes[:].bitcast(I32),
@@ -62,28 +58,52 @@ def tile_hotpatchcapsmodel_pa_kernel(
                 out=w2_plane[32 * quadrant : 32 * quadrant + 4, :].bitcast(I32),
                 in_=W2_scales[0, 4 * quadrant : 4 * quadrant + 4, :].bitcast(I32),
             )
-        for n in range(1, PAIRS):
-            nc.sync.dma_start(
-                out=h1_sb[:, PAIR * n : PAIR * (n + 1), :], in_=h1_rows[:, PAIR * n : PAIR * (n + 1), :]
-            )
-
-        b2_bc = keep.tile([P, E], BF16)
-        nc.scalar.dma_start(out=b2_bc[:], in_=b2.partition_broadcast(P))
-        nc.scalar.dma_start(out=small_rows[0:4, :], in_=ln_g.rearrange("(j c) -> j c", c=P))
-        nc.scalar.dma_start(out=small_rows[4:8, :], in_=ln_b.rearrange("(j c) -> j c", c=P))
-        nc.scalar.dma_start(out=small_rows[8:10, :], in_=pc_b.rearrange("(c n) q -> c (n q)", c=NP_TILES))
-        pcg_bc = keep.tile([P, NP], BF16)
-        nc.scalar.dma_start(out=pcg_bc[:], in_=pc_g.rearrange("n q -> (n q)").partition_broadcast(P))
-        pcbeta_bc = keep.tile([P, NP], BF16)
-        nc.scalar.dma_start(out=pcbeta_bc[:], in_=pc_beta.rearrange("n q -> (n q)").partition_broadcast(P))
+        nc.sync.dma_start(out=b2_rows[0:4, :], in_=b2.rearrange("(j c) -> j c", c=P))
+        nc.sync.dma_start(out=other_rows[0:2, :], in_=pc_g.rearrange("(c n) q -> c (n q)", c=NP_TILES))
+        nc.sync.dma_start(out=other_rows[2:4, :], in_=pc_beta.rearrange("(c n) q -> c (n q)", c=NP_TILES))
+        nc.sync.dma_start(out=other_rows[4:8, :], in_=ln_g.rearrange("(j c) -> j c", c=P))
+        nc.sync.dma_start(out=other_rows[8:12, :], in_=ln_b.rearrange("(j c) -> j c", c=P))
+        nc.sync.dma_start(out=other_rows[12:14, :], in_=pc_b.rearrange("(c n) q -> c (n q)", c=NP_TILES))
+        pw_sb = keep.tile([P, P * CAP_DIM], BF16)
+        nc.sync.dma_start(out=pw_sb[:], in_=pc_W.rearrange("n (j e) q -> (n j) (e q)", j=PACK))
+        for doubling in range(1, 4):
+            first = 2**doubling
+            nc.sync.dma_start(out=h1_sb[:, first : 2 * first, :], in_=h1_rows[:, first : 2 * first, :])
 
         warm = keep.tile([P, 1], F32)
         nc.scalar.activation(out=warm[:], in_=eps[:], func=ACT.Abs_reciprocal_sqrt)
 
-        ident_b = keep.tile([P, P], BF16)
-        make_identity(nc, ident_b[:])
         ident_f = keep.tile([P, P], F32)
         make_identity(nc, ident_f[:])
+        ident_b = keep.tile([P, P], BF16)
+        make_identity(nc, ident_b[:])
+
+        def to_columns(rows, count, tag):
+            rows_t = psum.tile([P, P], BF16, name="rows_t", tag=tag, bufs=2)
+            nc.tensor.transpose(rows_t[:], rows[:], ident_b[:])
+            columns = keep.tile([P, count], F32, name="columns_" + tag)
+            nc.vector.tensor_copy(out=columns[:], in_=rows_t[:, 0:count])
+            return columns
+
+        def along_free_axis(columns, tag):
+            repeated = keep.tile([P, 4, P], F32, name="repeated_" + tag)
+            nc.vector.tensor_copy(out=repeated[:], in_=columns.unsqueeze(2).to_broadcast([P, 4, P]))
+            spread = psum.tile([P, 4, P], F32, name="spread", tag=tag, bufs=2)
+            for k in range(4):
+                nc.tensor.transpose(spread[:, k, :], repeated[:, k, :], ident_f[:])
+            everywhere = keep.tile([P, 4 * P], F32, name="everywhere_" + tag)
+            nc.vector.tensor_copy(out=everywhere[:], in_=spread[:].rearrange("p k c -> p (k c)"))
+            return everywhere
+
+        b2_bc = along_free_axis(to_columns(b2_rows, 4, "normed_t")[:, 0:4], "normed_t")
+        others = to_columns(other_rows, 14, "centred")
+        gain_shift_bc = along_free_axis(others[:, 0:4], "centred")
+        pcg_bc = gain_shift_bc[:, 0:NP]
+        pcbeta_bc = gain_shift_bc[:, NP : 2 * NP]
+        ln_g_col = others[:, 4:8]
+        ln_b_col = others[:, 8:12]
+        pc_b_col = others[:, 12:14]
+
         same_capsule = keep.tile([P, P // CAP_DIM], F32)
         nc.vector.tensor_reduce(
             out=same_capsule[:], in_=ident_f[:].rearrange("p (n q) -> p n q", q=CAP_DIM), axis=AXIS.X, op=ALU.add
@@ -98,212 +118,12 @@ def tile_hotpatchcapsmodel_pa_kernel(
             op1=ALU.add,
         )
 
-        pw_t = psum.tile([P, CAP_DIM, P], BF16, tag="centred", bufs=2)
+        pw_t = psum.tile([P, CAP_DIM, P], BF16, tag="prim_t")
         pw_by_q = pw_sb[:].rearrange("p (e q) -> p e q", q=CAP_DIM)
         for q in range(CAP_DIM):
             nc.tensor.transpose(pw_t[:, q, :], pw_by_q[:, :, q], ident_b[:])
         pw_grouped = keep.tile([P, CAPS, CAP_DIM, PACK], BF16, align_bytes=64)
         nc.scalar.copy(out=pw_grouped[:], in_=pw_t[:].rearrange("p q (n j) -> p n q j", j=PACK))
-        small_rows_t = psum.tile([P, P], BF16, tag="centred", bufs=2)
-        nc.tensor.transpose(small_rows_t[:], small_rows[:], ident_b[:])
-
-        h1_t, h1_grouped, h1_codes, h1_plane = {}, {}, {}, {}
-        acc, z, z_sum, neg_mean, rstd = {}, {}, {}, {}, {}
-        normed, normed_t, h_t, h_codes, h_plane = {}, {}, {}, {}, {}
-        prim_t, biased_t, centred, g_squares, g_sq_sum, g_rstd, result = {}, {}, {}, {}, {}, {}, {}
-
-        def transpose_h1(n):
-            h1_t[n] = psum.tile([P, PAIR, 2, P], F32, name="h1_t", tag="h1_t")
-            for i in range(PAIR):
-                words = h1_sb[:, PAIR * n + i, :].bitcast(F32)
-                for u in range(2):
-                    nc.tensor.transpose(h1_t[n][:, i, u, :], words[:, u : H1 // 2 : 2], ident_f[:])
-
-        def group_h1(n):
-            h1_grouped[n] = work.tile([P, PAIR, P, PACK], BF16, name="h1_grouped", align_bytes=64)
-            nc.vector.tensor_copy(
-                out=h1_grouped[n][:].bitcast(F32), in_=h1_t[n][:].rearrange("p i u r -> p i r u")
-            )
-
-        def quantise_h1(n):
-            h1_codes[n] = work.tile([P, PAIR_ROWS], U32, name="h1_codes", align_bytes=64)
-            h1_plane[n] = work.tile([P, PAIR_ROWS], U8, name="h1_plane", align_bytes=64)
-            nc.vector.quantize_mx(
-                out=h1_codes[n][:].bitcast(FP8X4),
-                scales=h1_plane[n][:],
-                in_=h1_grouped[n][:].rearrange("p i r t -> p (i r t)"),
-            )
-
-        def embed(n):
-            for i in range(PAIR):
-                rows = slice(P * i, P * (i + 1))
-                acc[n, i] = psum.tile([P, E], F32, name="acc", tag="acc", bufs=2)
-                nc.tensor.matmul_mx(
-                    out=acc[n, i][:],
-                    lhsT=h1_codes[n][:, rows].bitcast(FP8X4),
-                    lhsT_scale=h1_plane[n][:, rows],
-                    rhs=w2_codes[:].bitcast(FP8X4),
-                    rhs_scale=w2_plane[:],
-                    start=True,
-                    stop=True,
-                )
-
-        def add_b2(n):
-            z[n] = work.tile([P, PAIR, E], F32, name="z")
-            for i in range(PAIR):
-                nc.vector.tensor_tensor(out=z[n][:, i, :], in0=acc[n, i][:], in1=b2_bc[:], op=ALU.add)
-
-        def relu_and_sum(n):
-            z_sum[n] = work.tile([P, PAIR], F32, name="z_sum")
-            for i in range(PAIR):
-                nc.scalar.activation(
-                    out=z[n][:, i, :], in_=z[n][:, i, :], func=ACT.Relu, accum_out=z_sum[n][:, i : i + 1]
-                )
-
-        def mean(n):
-            neg_mean[n] = work.tile([P, PAIR], F32, name="neg_mean")
-            nc.vector.tensor_scalar(
-                out=neg_mean[n][:], in0=z_sum[n][:], scalar1=-1.0 / E, scalar2=None, op0=ALU.mult
-            )
-
-        def variance(n):
-            sq_sum = work.tile([P, PAIR], F32)
-            for i in range(PAIR):
-                squares = work.tile([P, E], BF16)
-                nc.scalar.activation(
-                    out=squares[:],
-                    in_=z[n][:, i, :],
-                    func=ACT.Square,
-                    bias=neg_mean[n][:, i : i + 1],
-                    scale=1.0,
-                    accum_out=sq_sum[:, i : i + 1],
-                )
-            rstd[n] = work.tile([P, PAIR], F32, name="rstd")
-            nc.scalar.activation(
-                out=rstd[n][:], in_=sq_sum[:], func=ACT.Abs_reciprocal_sqrt, bias=eps[:], scale=1.0 / E
-            )
-
-        def normalise(n):
-            normed[n] = work.tile([P, PAIR, E], F32, name="normed")
-            for i in range(PAIR):
-                nc.vector.tensor_scalar(
-                    out=normed[n][:, i, :],
-                    in0=z[n][:, i, :],
-                    scalar1=neg_mean[n][:, i : i + 1],
-                    scalar2=rstd[n][:, i : i + 1],
-                    op0=ALU.add,
-                    op1=ALU.mult,
-                )
-
-        def transpose_normed(n):
-            for half in range(2):
-                normed_t[n, half] = psum.tile([P, 2, PAIR, P], F32, name="normed_t", tag="normed_t", bufs=2)
-                for jj in range(2):
-                    j = 2 * half + jj
-                    for i in range(PAIR):
-                        nc.tensor.transpose(
-                            normed_t[n, half][:, jj, i, :], normed[n][:, i, P * j : P * (j + 1)], ident_f[:]
-                        )
-
-        def gain_and_shift(n):
-            h_t[n] = work.tile([P, PACK, PAIR_ROWS], BF16, name="h_t")
-            for j in range(PACK):
-                nc.scalar.activation(
-                    out=h_t[n][:, j, :],
-                    in_=normed_t[n, j // 2][:, j % 2, :, :].rearrange("p i r -> p (i r)"),
-                    func=ACT.Identity,
-                    bias=columns[:, PACK + j : PACK + j + 1],
-                    scale=columns[:, j : j + 1],
-                )
-
-        def quantise_h(n):
-            h_grouped = work.tile([P, PAIR_ROWS, PACK], BF16, align_bytes=64)
-            nc.vector.tensor_copy(
-                out=h_grouped[:].rearrange("p (c x) j -> p c j x", x=4),
-                in_=h_t[n][:].rearrange("p j (c x) -> p c j x", x=4),
-            )
-            h_codes[n] = work.tile([P, PAIR_ROWS], U32, name="h_codes", align_bytes=64)
-            h_plane[n] = work.tile([P, PAIR_ROWS], U8, name="h_plane", align_bytes=64)
-            nc.vector.quantize_mx(
-                out=h_codes[n][:].bitcast(FP8X4),
-                scales=h_plane[n][:],
-                in_=h_grouped[:].rearrange("p r j -> p (r j)"),
-            )
-
-        def capsules(n):
-            prim_t[n] = psum.tile([P, NP_TILES, PAIR_ROWS], F32, name="prim_t", tag="prim_t")
-            for c in range(NP_TILES):
-                cols = slice(P * c, P * (c + 1))
-                nc.tensor.matmul_mx(
-                    out=prim_t[n][:, c, :],
-                    lhsT=pw_codes[:, cols].bitcast(FP8X4),
-                    lhsT_scale=pw_plane[:, cols],
-                    rhs=h_codes[n][:].bitcast(FP8X4),
-                    rhs_scale=h_plane[n][:],
-                    start=True,
-                    stop=True,
-                )
-
-        def add_pc_b(n):
-            biased_t[n] = work.tile([P, NP_TILES, PAIR_ROWS], F32, name="biased_t")
-            for c in range(NP_TILES):
-                nc.scalar.activation(
-                    out=biased_t[n][:, c, :],
-                    in_=prim_t[n][:, c, :],
-                    func=ACT.Identity,
-                    bias=columns[:, 2 * PACK + c : 2 * PACK + c + 1],
-                    scale=1.0,
-                )
-
-        def centre_and_transpose(n):
-            centred[n] = psum.tile([P, PAIR, NP], F32, name="centred", tag="centred", bufs=2)
-            for i in range(PAIR):
-                for c in range(NP_TILES):
-                    nc.tensor.matmul(
-                        out=centred[n][:, i, P * c : P * (c + 1)],
-                        lhsT=biased_t[n][:, c, P * i : P * (i + 1)],
-                        rhs=centre[:],
-                        start=True,
-                        stop=True,
-                    )
-
-        def square(n):
-            g_squares[n] = work.tile([P, GROUPS, CAP_DIM], F32, name="g_squares")
-            nc.scalar.activation(
-                out=g_squares[n][:].rearrange("p g q -> p (g q)"),
-                in_=centred[n][:].rearrange("p i c -> p (i c)"),
-                func=ACT.Square,
-            )
-
-        def sum_squares(n):
-            g_sq_sum[n] = work.tile([P, GROUPS], F32, name="g_sq_sum")
-            nc.vector.tensor_reduce(out=g_sq_sum[n][:], in_=g_squares[n][:], axis=AXIS.X, op=ALU.add)
-
-        def capsule_rstd(n):
-            g_rstd[n] = work.tile([P, GROUPS], F32, name="g_rstd")
-            nc.scalar.activation(
-                out=g_rstd[n][:], in_=g_sq_sum[n][:], func=ACT.Abs_reciprocal_sqrt, bias=eps[:], scale=1.0 / CAP_DIM
-            )
-
-        def scale_capsules(n):
-            result[n] = work.tile([P, PAIR, NP], F32, name="result")
-            nc.vector.tensor_tensor(
-                out=result[n][:].rearrange("p i (n q) -> p (i n) q", q=CAP_DIM),
-                in0=centred[n][:].rearrange("p i (n q) -> p (i n) q", q=CAP_DIM),
-                in1=g_rstd[n][:].unsqueeze(2).to_broadcast([P, GROUPS, CAP_DIM]),
-                op=ALU.mult,
-            )
-
-        def finish(n):
-            over_pair = [P, PAIR, NP]
-            nc.vector.tensor_tensor(
-                out=result[n][:], in0=result[n][:], in1=pcg_bc[:].unsqueeze(1).to_broadcast(over_pair), op=ALU.mult
-            )
-            nc.vector.tensor_tensor(
-                out=result[n][:], in0=result[n][:], in1=pcbeta_bc[:].unsqueeze(1).to_broadcast(over_pair), op=ALU.add
-            )
-            nc.sync.dma_start(out=out_rows[:, PAIR * n : PAIR * (n + 1), :], in_=result[n][:])
-
         pw_codes = keep.tile([P, NP], U32, align_bytes=64)
         pw_plane = keep.tile([P, NP], U8, align_bytes=64)
         nc.vector.quantize_mx(
@@ -311,27 +131,123 @@ def tile_hotpatchcapsmodel_pa_kernel(
             scales=pw_plane[:],
             in_=pw_grouped[:].rearrange("p n q j -> p (n q j)"),
         )
-        columns = keep.tile([P, 2 * PACK + NP_TILES], F32)
-        nc.vector.tensor_copy(out=columns[:], in_=small_rows_t[:, 0 : 2 * PACK + NP_TILES])
 
-        for n in range(PAIRS):
-            transpose_h1(n)
-            group_h1(n)
-            quantise_h1(n)
-            embed(n)
-            add_b2(n)
-            relu_and_sum(n)
-            mean(n)
-            variance(n)
-            normalise(n)
-            transpose_normed(n)
-            gain_and_shift(n)
-            quantise_h(n)
-            capsules(n)
-            add_pc_b(n)
-            centre_and_transpose(n)
-            square(n)
-            sum_squares(n)
-            capsule_rstd(n)
-            scale_capsules(n)
-            finish(n)
+        for t in range(TILES):
+            h1_t = psum.tile([P, 2, P], F32, tag="h1_t")
+            words = h1_sb[:, t, :].bitcast(F32)
+            for u in range(2):
+                nc.tensor.transpose(h1_t[:, u, :], words[:, u : H1 // 2 : 2], ident_f[:])
+            h1_grouped = work.tile([P, P, PACK], BF16, align_bytes=64)
+            nc.vector.tensor_copy(out=h1_grouped[:].bitcast(F32), in_=h1_t[:].rearrange("p u r -> p r u"))
+            h1_codes = work.tile([P, P], U32, align_bytes=64)
+            h1_plane = work.tile([P, P], U8, align_bytes=64)
+            nc.vector.quantize_mx(
+                out=h1_codes[:].bitcast(FP8X4),
+                scales=h1_plane[:],
+                in_=h1_grouped[:].rearrange("p r k -> p (r k)"),
+            )
+
+            acc = psum.tile([P, E], F32, tag="acc", bufs=2)
+            nc.tensor.matmul_mx(
+                out=acc[:],
+                lhsT=h1_codes[:].bitcast(FP8X4),
+                lhsT_scale=h1_plane[:],
+                rhs=w2_codes[:].bitcast(FP8X4),
+                rhs_scale=w2_plane[:],
+                start=True,
+                stop=True,
+            )
+            z = work.tile([P, E], F32)
+            nc.vector.tensor_tensor(out=z[:], in0=acc[:], in1=b2_bc[:], op=ALU.add)
+            z_sum = work.tile([P, 1], F32)
+            nc.scalar.activation(out=z[:], in_=z[:], func=ACT.Relu, accum_out=z_sum[:])
+
+            squares = work.tile([P, E], BF16)
+            sq_sum = work.tile([P, 1], F32)
+            nc.scalar.activation(
+                out=squares[:], in_=z[:], func=ACT.Square, bias=z_sum[:], scale=-float(E), accum_out=sq_sum[:]
+            )
+            rstd = work.tile([P, 1], F32)
+            nc.scalar.activation(
+                out=rstd[:], in_=sq_sum[:], func=ACT.Abs_reciprocal_sqrt, bias=eps[:], scale=1.0 / float(E) ** 3
+            )
+            neg_mean = work.tile([P, 1], F32)
+            nc.vector.tensor_scalar(out=neg_mean[:], in0=z_sum[:], scalar1=-1.0 / E, scalar2=None, op0=ALU.mult)
+            normed = work.tile([P, E], F32)
+            nc.vector.tensor_scalar(
+                out=normed[:], in0=z[:], scalar1=neg_mean[:], scalar2=rstd[:], op0=ALU.add, op1=ALU.mult
+            )
+
+            normed_t = psum.tile([P, PACK, P], F32, tag="normed_t", bufs=2)
+            for j in range(PACK):
+                nc.tensor.transpose(normed_t[:, j, :], normed[:, P * j : P * (j + 1)], ident_f[:])
+            h_t = work.tile([P, PACK, P], BF16)
+            for j in range(PACK):
+                nc.scalar.activation(
+                    out=h_t[:, j, :],
+                    in_=normed_t[:, j, :],
+                    func=ACT.Identity,
+                    bias=ln_b_col[:, j : j + 1],
+                    scale=ln_g_col[:, j : j + 1],
+                )
+            h_grouped = work.tile([P, P, PACK], BF16, align_bytes=64)
+            nc.vector.tensor_copy(
+                out=h_grouped[:].rearrange("p (c x) j -> p c j x", x=4),
+                in_=h_t[:].rearrange("p j (c x) -> p c j x", x=4),
+            )
+            h_codes = work.tile([P, P], U32, align_bytes=64)
+            h_plane = work.tile([P, P], U8, align_bytes=64)
+            nc.vector.quantize_mx(
+                out=h_codes[:].bitcast(FP8X4),
+                scales=h_plane[:],
+                in_=h_grouped[:].rearrange("p r j -> p (r j)"),
+            )
+
+            prim_t = psum.tile([P, NP_TILES, P], F32, tag="prim_t")
+            biased_t = work.tile([P, NP_TILES, P], F32)
+            for c in range(NP_TILES):
+                cols = slice(P * c, P * (c + 1))
+                nc.tensor.matmul_mx(
+                    out=prim_t[:, c, :],
+                    lhsT=pw_codes[:, cols].bitcast(FP8X4),
+                    lhsT_scale=pw_plane[:, cols],
+                    rhs=h_codes[:].bitcast(FP8X4),
+                    rhs_scale=h_plane[:],
+                    start=True,
+                    stop=True,
+                )
+            for c in range(NP_TILES):
+                nc.scalar.activation(
+                    out=biased_t[:, c, :],
+                    in_=prim_t[:, c, :],
+                    func=ACT.Identity,
+                    bias=pc_b_col[:, c : c + 1],
+                    scale=1.0,
+                )
+
+            centred = psum.tile([P, CAPS, CAP_DIM], F32, tag="centred", bufs=2)
+            centred_flat = centred[:].rearrange("p n q -> p (n q)")
+            for c in range(NP_TILES):
+                nc.tensor.matmul(
+                    out=centred_flat[:, P * c : P * (c + 1)], lhsT=biased_t[:, c, :], rhs=centre[:], start=True, stop=True
+                )
+
+            cap_squares = work.tile([P, CAPS, CAP_DIM], F32)
+            nc.scalar.activation(out=cap_squares[:], in_=centred[:], func=ACT.Square)
+            cap_sq_sum = work.tile([P, CAPS], F32)
+            nc.vector.tensor_reduce(out=cap_sq_sum[:], in_=cap_squares[:], axis=AXIS.X, op=ALU.add)
+            cap_rstd = work.tile([P, CAPS], F32)
+            nc.scalar.activation(
+                out=cap_rstd[:], in_=cap_sq_sum[:], func=ACT.Abs_reciprocal_sqrt, bias=eps[:], scale=1.0 / CAP_DIM
+            )
+            result = work.tile([P, CAPS, CAP_DIM], F32)
+            nc.vector.tensor_tensor(
+                out=result[:],
+                in0=centred[:],
+                in1=cap_rstd[:].unsqueeze(2).to_broadcast([P, CAPS, CAP_DIM]),
+                op=ALU.mult,
+            )
+            result_flat = result[:].rearrange("p n q -> p (n q)")
+            nc.gpsimd.tensor_tensor(out=result_flat, in0=result_flat, in1=pcg_bc, op=ALU.mult)
+            nc.gpsimd.tensor_tensor(out=result_flat, in0=result_flat, in1=pcbeta_bc, op=ALU.add)
+            nc.sync.dma_start(out=out_rows[:, t, :], in_=result_flat)

from contextlib import ExitStack

import concourse.mybir as mybir
from concourse.masks import make_identity

F32 = mybir.dt.float32
BF16 = mybir.dt.bfloat16
I32 = mybir.dt.int32
U32 = mybir.dt.uint32
U8 = mybir.dt.uint8
FP8X4 = mybir.dt.float8_e4m3fn_x4
ALU = mybir.AluOpType
ACT = mybir.ActivationFunctionType
AXIS = mybir.AxisListType

P = 128
PACK = 4
B, H1, E = 2048, 512, 512
CAPS, CAP_DIM = 32, 8
NP = CAPS * CAP_DIM
NP_TILES = NP // P
TILES = B // P
EPS = 1e-5

FLOPS = 2 * B * H1 * E + 2 * B * E * NP


def tile_hotpatchcapsmodel_pa_kernel(
    tc, h1, W2_words, W2_scales, b2, ln_g, ln_b, pc_W, pc_b, pc_g, pc_beta, out
):
    nc = tc.nc
    with ExitStack() as ctx:
        keep = ctx.enter_context(tc.tile_pool(name="keep", bufs=1))
        work = ctx.enter_context(tc.tile_pool(name="work", bufs=4))
        psum = ctx.enter_context(tc.psum_pool(name="psum", bufs=1))

        h1_rows = h1.rearrange("(p t) k -> p t k", t=TILES)
        out_rows = out.rearrange("(p t) n q -> p t (n q)", t=TILES)

        w2_plane = keep.tile([P, E], U8, align_bytes=64)
        nc.vector.memset(w2_plane[:].bitcast(I32), 0)
        b2_rows = keep.tile([P, P], BF16)
        nc.vector.memset(b2_rows[:], 0.0)
        other_rows = keep.tile([P, P], BF16)
        nc.vector.memset(other_rows[:], 0.0)
        eps = keep.tile([P, 1], F32)
        nc.vector.memset(eps[:], EPS)

        h1_sb = keep.tile([P, TILES, H1], BF16)
        nc.sync.dma_start(out=h1_sb[:, 0:2, :], in_=h1_rows[:, 0:2, :])
        w2_codes = keep.tile([P, E], U32, align_bytes=64)
        nc.sync.dma_start(
            out=w2_codes[:].bitcast(I32),
            in_=W2_words[0].rearrange("p n t -> p (n t)").bitcast(I32),
        )
        for quadrant in range(4):
            nc.sync.dma_start(
                out=w2_plane[32 * quadrant : 32 * quadrant + 4, :].bitcast(I32),
                in_=W2_scales[0, 4 * quadrant : 4 * quadrant + 4, :].bitcast(I32),
            )
        nc.sync.dma_start(out=b2_rows[0:4, :], in_=b2.rearrange("(j c) -> j c", c=P))
        nc.sync.dma_start(out=other_rows[0:2, :], in_=pc_g.rearrange("(c n) q -> c (n q)", c=NP_TILES))
        nc.sync.dma_start(out=other_rows[2:4, :], in_=pc_beta.rearrange("(c n) q -> c (n q)", c=NP_TILES))
        nc.sync.dma_start(out=other_rows[4:8, :], in_=ln_g.rearrange("(j c) -> j c", c=P))
        nc.sync.dma_start(out=other_rows[8:12, :], in_=ln_b.rearrange("(j c) -> j c", c=P))
        nc.sync.dma_start(out=other_rows[12:14, :], in_=pc_b.rearrange("(c n) q -> c (n q)", c=NP_TILES))
        pw_sb = keep.tile([P, P * CAP_DIM], BF16)
        nc.sync.dma_start(out=pw_sb[:], in_=pc_W.rearrange("n (j e) q -> (n j) (e q)", j=PACK))
        for doubling in range(1, 4):
            first = 2**doubling
            nc.sync.dma_start(out=h1_sb[:, first : 2 * first, :], in_=h1_rows[:, first : 2 * first, :])

        warm = keep.tile([P, 1], F32)
        nc.scalar.activation(out=warm[:], in_=eps[:], func=ACT.Abs_reciprocal_sqrt)

        ident_f = keep.tile([P, P], F32)
        make_identity(nc, ident_f[:])
        ident_b = keep.tile([P, P], BF16)
        make_identity(nc, ident_b[:])

        def to_columns(rows, count, tag):
            rows_t = psum.tile([P, P], BF16, name="rows_t", tag=tag, bufs=2)
            nc.tensor.transpose(rows_t[:], rows[:], ident_b[:])
            columns = keep.tile([P, count], F32, name="columns_" + tag)
            nc.vector.tensor_copy(out=columns[:], in_=rows_t[:, 0:count])
            return columns

        def along_free_axis(columns, tag):
            repeated = keep.tile([P, 4, P], F32, name="repeated_" + tag)
            nc.vector.tensor_copy(out=repeated[:], in_=columns.unsqueeze(2).to_broadcast([P, 4, P]))
            spread = psum.tile([P, 4, P], F32, name="spread", tag=tag, bufs=2)
            for k in range(4):
                nc.tensor.transpose(spread[:, k, :], repeated[:, k, :], ident_f[:])
            everywhere = keep.tile([P, 4 * P], F32, name="everywhere_" + tag)
            nc.vector.tensor_copy(out=everywhere[:], in_=spread[:].rearrange("p k c -> p (k c)"))
            return everywhere

        b2_bc = along_free_axis(to_columns(b2_rows, 4, "normed_t")[:, 0:4], "normed_t")
        others = to_columns(other_rows, 14, "centred")
        gain_shift_bc = along_free_axis(others[:, 0:4], "centred")
        pcg_bc = gain_shift_bc[:, 0:NP]
        pcbeta_bc = gain_shift_bc[:, NP : 2 * NP]
        ln_g_col = others[:, 4:8]
        ln_b_col = others[:, 8:12]
        pc_b_col = others[:, 12:14]

        same_capsule = keep.tile([P, P // CAP_DIM], F32)
        nc.vector.tensor_reduce(
            out=same_capsule[:], in_=ident_f[:].rearrange("p (n q) -> p n q", q=CAP_DIM), axis=AXIS.X, op=ALU.add
        )
        centre = keep.tile([P, P], F32)
        nc.vector.scalar_tensor_tensor(
            out=centre[:].rearrange("p (n q) -> p n q", q=CAP_DIM),
            in0=same_capsule[:].unsqueeze(2).to_broadcast([P, P // CAP_DIM, CAP_DIM]),
            scalar=-1.0 / CAP_DIM,
            in1=ident_f[:].rearrange("p (n q) -> p n q", q=CAP_DIM),
            op0=ALU.mult,
            op1=ALU.add,
        )

        pw_t = psum.tile([P, CAP_DIM, P], BF16, tag="prim_t")
        pw_by_q = pw_sb[:].rearrange("p (e q) -> p e q", q=CAP_DIM)
        for q in range(CAP_DIM):
            nc.tensor.transpose(pw_t[:, q, :], pw_by_q[:, :, q], ident_b[:])
        pw_grouped = keep.tile([P, CAPS, CAP_DIM, PACK], BF16, align_bytes=64)
        nc.scalar.copy(out=pw_grouped[:], in_=pw_t[:].rearrange("p q (n j) -> p n q j", j=PACK))
        pw_codes = keep.tile([P, NP], U32, align_bytes=64)
        pw_plane = keep.tile([P, NP], U8, align_bytes=64)
        nc.vector.quantize_mx(
            out=pw_codes[:].bitcast(FP8X4),
            scales=pw_plane[:],
            in_=pw_grouped[:].rearrange("p n q j -> p (n q j)"),
        )

        for t in range(TILES):
            h1_t = psum.tile([P, 2, P], F32, tag="h1_t")
            words = h1_sb[:, t, :].bitcast(F32)
            for u in range(2):
                nc.tensor.transpose(h1_t[:, u, :], words[:, u : H1 // 2 : 2], ident_f[:])
            h1_grouped = work.tile([P, P, PACK], BF16, align_bytes=64)
            nc.vector.tensor_copy(out=h1_grouped[:].bitcast(F32), in_=h1_t[:].rearrange("p u r -> p r u"))
            h1_codes = work.tile([P, P], U32, align_bytes=64)
            h1_plane = work.tile([P, P], U8, align_bytes=64)
            nc.vector.quantize_mx(
                out=h1_codes[:].bitcast(FP8X4),
                scales=h1_plane[:],
                in_=h1_grouped[:].rearrange("p r k -> p (r k)"),
            )

            acc = psum.tile([P, E], F32, tag="acc", bufs=2)
            nc.tensor.matmul_mx(
                out=acc[:],
                lhsT=h1_codes[:].bitcast(FP8X4),
                lhsT_scale=h1_plane[:],
                rhs=w2_codes[:].bitcast(FP8X4),
                rhs_scale=w2_plane[:],
                start=True,
                stop=True,
            )
            z = work.tile([P, E], F32)
            nc.vector.tensor_tensor(out=z[:], in0=acc[:], in1=b2_bc[:], op=ALU.add)
            z_sum = work.tile([P, 1], F32)
            nc.scalar.activation(out=z[:], in_=z[:], func=ACT.Relu, accum_out=z_sum[:])

            squares = work.tile([P, E], BF16)
            sq_sum = work.tile([P, 1], F32)
            nc.scalar.activation(
                out=squares[:], in_=z[:], func=ACT.Square, bias=z_sum[:], scale=-float(E), accum_out=sq_sum[:]
            )
            rstd = work.tile([P, 1], F32)
            nc.scalar.activation(
                out=rstd[:], in_=sq_sum[:], func=ACT.Abs_reciprocal_sqrt, bias=eps[:], scale=1.0 / float(E) ** 3
            )
            neg_mean = work.tile([P, 1], F32)
            nc.vector.tensor_scalar(out=neg_mean[:], in0=z_sum[:], scalar1=-1.0 / E, scalar2=None, op0=ALU.mult)
            normed = work.tile([P, E], F32)
            nc.vector.tensor_scalar(
                out=normed[:], in0=z[:], scalar1=neg_mean[:], scalar2=rstd[:], op0=ALU.add, op1=ALU.mult
            )

            normed_t = psum.tile([P, PACK, P], F32, tag="normed_t", bufs=2)
            for j in range(PACK):
                nc.tensor.transpose(normed_t[:, j, :], normed[:, P * j : P * (j + 1)], ident_f[:])
            h_t = work.tile([P, PACK, P], BF16)
            for j in range(PACK):
                nc.scalar.activation(
                    out=h_t[:, j, :],
                    in_=normed_t[:, j, :],
                    func=ACT.Identity,
                    bias=ln_b_col[:, j : j + 1],
                    scale=ln_g_col[:, j : j + 1],
                )
            h_grouped = work.tile([P, P, PACK], BF16, align_bytes=64)
            nc.vector.tensor_copy(
                out=h_grouped[:].rearrange("p (c x) j -> p c j x", x=4),
                in_=h_t[:].rearrange("p j (c x) -> p c j x", x=4),
            )
            h_codes = work.tile([P, P], U32, align_bytes=64)
            h_plane = work.tile([P, P], U8, align_bytes=64)
            nc.vector.quantize_mx(
                out=h_codes[:].bitcast(FP8X4),
                scales=h_plane[:],
                in_=h_grouped[:].rearrange("p r j -> p (r j)"),
            )

            prim_t = psum.tile([P, NP_TILES, P], F32, tag="prim_t")
            biased_t = work.tile([P, NP_TILES, P], F32)
            for c in range(NP_TILES):
                cols = slice(P * c, P * (c + 1))
                nc.tensor.matmul_mx(
                    out=prim_t[:, c, :],
                    lhsT=pw_codes[:, cols].bitcast(FP8X4),
                    lhsT_scale=pw_plane[:, cols],
                    rhs=h_codes[:].bitcast(FP8X4),
                    rhs_scale=h_plane[:],
                    start=True,
                    stop=True,
                )
            for c in range(NP_TILES):
                nc.scalar.activation(
                    out=biased_t[:, c, :],
                    in_=prim_t[:, c, :],
                    func=ACT.Identity,
                    bias=pc_b_col[:, c : c + 1],
                    scale=1.0,
                )

            centred = psum.tile([P, CAPS, CAP_DIM], F32, tag="centred", bufs=2)
            centred_flat = centred[:].rearrange("p n q -> p (n q)")
            for c in range(NP_TILES):
                nc.tensor.matmul(
                    out=centred_flat[:, P * c : P * (c + 1)], lhsT=biased_t[:, c, :], rhs=centre[:], start=True, stop=True
                )

            cap_squares = work.tile([P, CAPS, CAP_DIM], F32)
            nc.scalar.activation(out=cap_squares[:], in_=centred[:], func=ACT.Square)
            cap_sq_sum = work.tile([P, CAPS], F32)
            nc.vector.tensor_reduce(out=cap_sq_sum[:], in_=cap_squares[:], axis=AXIS.X, op=ALU.add)
            cap_rstd = work.tile([P, CAPS], F32)
            nc.scalar.activation(
                out=cap_rstd[:], in_=cap_sq_sum[:], func=ACT.Abs_reciprocal_sqrt, bias=eps[:], scale=1.0 / CAP_DIM
            )
            result = work.tile([P, CAPS, CAP_DIM], F32)
            nc.vector.tensor_tensor(
                out=result[:],
                in0=centred[:],
                in1=cap_rstd[:].unsqueeze(2).to_broadcast([P, CAPS, CAP_DIM]),
                op=ALU.mult,
            )
            result_flat = result[:].rearrange("p n q -> p (n q)")
            nc.gpsimd.tensor_tensor(out=result_flat, in0=result_flat, in1=pcg_bc, op=ALU.mult)
            nc.gpsimd.tensor_tensor(out=result_flat, in0=result_flat, in1=pcbeta_bc, op=ALU.add)
            nc.sync.dma_start(out=out_rows[:, t, :], in_=result_flat)
